import numpy as np
import ml_dtypes


def mxq(x, axis, fmt="e4m3"):
    dtype, down = {"e4m3": (ml_dtypes.float8_e4m3fn, 7), "e5m2": (ml_dtypes.float8_e5m2, 14)}[fmt]
    v = np.moveaxis(np.asarray(x, np.float32).astype(ml_dtypes.bfloat16).astype(np.float64), axis, -1)
    blocks = v.reshape(v.shape[:-1] + (-1, 32))
    amax = np.abs(blocks).max(-1, keepdims=True)
    byte = np.maximum(np.where(amax > 0, np.frexp(amax)[1] - 1 + 127, 0) - down, 1)
    scale = np.exp2(byte - 127.0)
    codes = (blocks / scale).astype(np.float32).astype(dtype).astype(np.float64)
    return np.moveaxis((codes * scale).reshape(v.shape), -1, axis)


WIDE = False


def mx_kscale(k):
    if not WIDE:
        return np.ones(k)
    levels = np.array([10, -10, 5, -5, 0])
    a = np.random.permutation(np.resize(levels, k // 512 * 4)).reshape(k // 512, 4)
    idx = np.arange(k)
    return np.exp2(a[idx // 512, idx % 128 // 32])


BF16 = ml_dtypes.bfloat16


def bf(x):
    return np.asarray(x, np.float32).astype(BF16)


def f64(x):
    return np.asarray(x).astype(np.float64)


B, CK, CV, NOBJ, T, H, W = 1, 128, 256, 2, 64, 16, 16
N = T * H * W
P = H * W
V = NOBJ * CV


def setup_inputs():
    s = mx_kscale(N)
    a = np.log2(s) - np.log2(s).min()
    g = np.exp2(np.round(np.log2(np.mean(1.0 / s))))
    ms = bf(1.0 + 0.5 * np.random.random((B, T, H, W)))[:, None]
    qe = np.random.random((B, CK, H, W))
    qe[:, 0] = 1.0
    m2 = np.random.standard_normal((B, CK, T, H, W)) ** 2
    m2[:, 0] += (a * np.log(2.0) * np.sqrt(CK)).reshape(T, H, W) / f64(ms)[:, 0]
    return {
        "query_key": bf(np.random.standard_normal((B, CK, H, W))),
        "query_selection": bf(qe),
        "qk_sel": bf(np.random.standard_normal((B, CK, H, W)) * np.random.random((B, CK, H, W))),
        "memory_key": bf(np.random.standard_normal((B, CK, T, H, W))),
        "mk_sq": bf(m2),
        "memory_shrinkage": ms,
        "memory_value": bf(2.0 * np.random.standard_normal((B, NOBJ, CV, T, H, W)) * (s * g).reshape(T, H, W)),
    }


def reference(query_key, query_selection, qk_sel, memory_key, mk_sq, memory_shrinkage, memory_value):
    qk = f64(query_key).reshape(B, CK, P)
    qe = f64(query_selection).reshape(B, CK, P)
    qs = f64(qk_sel).reshape(B, CK, P)
    mk = f64(memory_key).reshape(B, CK, N)
    m2 = f64(mk_sq).reshape(B, CK, N)
    ms = f64(memory_shrinkage).reshape(B, N)
    mv = f64(memory_value).reshape(B, V, N)
    a_sq = m2.transpose(0, 2, 1) @ qe
    two_ab = 2.0 * (mk.transpose(0, 2, 1) @ qs)
    b_sq = np.sum(qe * qk * qk, axis=1, keepdims=True)
    sim = (two_ab - a_sq - b_sq) * ms[:, :, None] * (1.0 / np.sqrt(CK))
    e = np.exp(sim - sim.max(axis=1, keepdims=True))
    mem = (mxq(mv, 2, "e4m3") @ mxq(e, 1, "e4m3")) / e.sum(axis=1, keepdims=True)
    return mem.reshape(B, NOBJ, CV, H, W)

@@ -1,0 +1,300 @@
+import math
+from contextlib import ExitStack
+
+import concourse.mybir as mybir
+from concourse.masks import make_identity
+
+F32 = mybir.dt.float32
+BF16 = mybir.dt.bfloat16
+U32 = mybir.dt.uint32
+U8 = mybir.dt.uint8
+FP8X4 = mybir.dt.float8_e4m3fn_x4
+ALU = mybir.AluOpType
+ACT = mybir.ActivationFunctionType
+AXIS = mybir.AxisListType
+
+P = 128
+CK = 128
+PIX = 256
+PIX_TILES = PIX // P
+SLOTS = 16384
+VAL = 512
+VAL_TILES = VAL // P
+HALF_VAL = VAL // 2
+K_PASS = 4 * P
+PASSES = SLOTS // K_PASS
+CHUNK = 2048
+CHUNKS = SLOTS // CHUNK
+PASSES_PER_CHUNK = CHUNK // K_PASS
+LEAD = 2
+INV_SQRT_CK = 1.0 / math.sqrt(CK)
+
+FLOPS = 2 * SLOTS * PIX * (2 * CK + VAL)
+
+
+def tile_xmem_pa_k_kernel(
+    tc,
+    query_key,
+    query_selection,
+    qk_sel,
+    memory_key,
+    mk_sq,
+    memory_shrinkage,
+    memory_value,
+    out,
+):
+    nc = tc.nc
+
+    qk_dram = query_key.rearrange("b c h w -> (b c) (h w)")
+    qe_dram = query_selection.rearrange("b c h w -> (b c) (h w)")
+    qs_dram = qk_sel.rearrange("b c h w -> (b c) (h w)")
+    mk_dram = memory_key.rearrange("b c t h w -> (b c) (t h w)")
+    m2_dram = mk_sq.rearrange("b c t h w -> (b c) (t h w)")
+    ms_dram = memory_shrinkage.rearrange("b o t h w -> (b o t h w)")
+    mv_dram = memory_value.rearrange("b o c t h w -> (b o c) (t h w)").rearrange(
+        "(q r) n -> r q n", r=P
+    )
+    out_dram = out.rearrange("b o c h w -> (b o c) (h w)").rearrange("(q r) p -> r q p", r=P)
+
+    with ExitStack() as whole:
+        const = whole.enter_context(tc.tile_pool(name="const", bufs=1))
+        sim_pool = whole.enter_context(tc.tile_pool(name="sim", bufs=1))
+        early_pool = whole.enter_context(tc.tile_pool(name="early", bufs=1))
+        raw_pool = whole.enter_context(tc.tile_pool(name="raw", bufs=4))
+        grouped_pool = whole.enter_context(tc.tile_pool(name="grouped", bufs=3))
+        psum_val = whole.enter_context(tc.psum_pool(name="psum_val", bufs=4))
+
+        ident_f32 = const.tile([P, P], F32)
+        make_identity(nc, ident_f32[:])
+        ident_bf16 = const.tile([P, P], BF16)
+        make_identity(nc, ident_bf16[:])
+
+        warm = const.tile([P, 1], F32)
+        nc.vector.memset(warm[:], 0.0)
+        nc.scalar.activation(out=warm[:], in_=warm[:], func=ACT.Exp)
+
+        qs_sb = const.tile([P, PIX], BF16)
+        nc.sync.dma_start(out=qs_sb[:], in_=qs_dram)
+        qe_sb = const.tile([P, PIX], BF16)
+        nc.sync.dma_start(out=qe_sb[:], in_=qe_dram)
+        qk_sb = const.tile([P, PIX], BF16)
+        nc.sync.dma_start(out=qk_sb[:], in_=qk_dram)
+
+        qs_twice = const.tile([P, PIX], BF16)
+        nc.vector.tensor_scalar(
+            out=qs_twice[:], in0=qs_sb[:], scalar1=2.0, scalar2=None, op0=ALU.mult
+        )
+        qe_minus = const.tile([P, PIX], BF16)
+        nc.vector.tensor_scalar(
+            out=qe_minus[:], in0=qe_sb[:], scalar1=-1.0, scalar2=None, op0=ALU.mult
+        )
+
+        def load_values(g):
+            raw = raw_pool.tile([P, VAL_TILES, K_PASS], BF16)
+            nc.sync.dma_start(out=raw[:], in_=mv_dram[:, :, g * K_PASS : (g + 1) * K_PASS])
+            return raw
+
+        def transpose_values(raw, grouped):
+            pairs = grouped[:].rearrange("i (v u) -> i v u", u=2)
+            for h in range(VAL // HALF_VAL):
+                bank = psum_val.tile([P, 2, HALF_VAL], F32)
+                for u in range(2):
+                    for q in range(HALF_VAL // P):
+                        words = raw[:, h * (HALF_VAL // P) + q, :].bitcast(F32)
+                        nc.tensor.transpose(
+                            bank[:, u, q * P : (q + 1) * P],
+                            words[:, u * P : (u + 1) * P],
+                            ident_f32[:],
+                        )
+                nc.scalar.copy(
+                    out=pairs[:, h * HALF_VAL : (h + 1) * HALF_VAL, :],
+                    in_=bank[:].rearrange("i u v -> i v u"),
+                )
+
+        w = [
+            [sim_pool.tile([P, CHUNK], F32, name="w%d_%d" % (pt, j)) for j in range(CHUNKS)]
+            for pt in range(PIX_TILES)
+        ]
+        chunk_max = const.tile([P, PIX_TILES, CHUNKS], F32)
+        chunk_sum = const.tile([P, PIX_TILES, CHUNKS], F32)
+        early = [
+            early_pool.tile([P, 2 * VAL], F32, name="early%d" % j, align_bytes=64)
+            for j in range(CHUNKS)
+        ]
+
+        with ExitStack() as phase:
+            stream = phase.enter_context(tc.tile_pool(name="stream", bufs=2))
+            psum_sim = phase.enter_context(tc.psum_pool(name="psum_sim", bufs=4))
+
+            qk_sq = const.tile([P, PIX], F32)
+            nc.vector.tensor_tensor(out=qk_sq[:], in0=qk_sb[:], in1=qk_sb[:], op=ALU.mult)
+            b_terms = const.tile([P, PIX], F32)
+            nc.vector.tensor_tensor(out=b_terms[:], in0=qk_sq[:], in1=qe_sb[:], op=ALU.mult)
+            b_bank = psum_sim.tile([P, PIX_TILES, P], F32, tag="u")
+            for pt in range(PIX_TILES):
+                nc.tensor.transpose(
+                    b_bank[:, pt, :], b_terms[:, pt * P : (pt + 1) * P], ident_f32[:]
+                )
+            b_sq = const.tile([P, PIX_TILES], F32)
+            nc.vector.reduce_sum(out=b_sq[:], in_=b_bank[:], axis=AXIS.X)
+
+            for j in range(CHUNKS):
+                slots = slice(j * CHUNK, (j + 1) * CHUNK)
+                mk_sb = stream.tile([P, CHUNK], BF16)
+                nc.sync.dma_start(out=mk_sb[:], in_=mk_dram[:, slots])
+                m2_sb = stream.tile([P, CHUNK], BF16)
+                nc.sync.dma_start(out=m2_sb[:], in_=m2_dram[:, slots])
+                ms_sb = stream.tile([P, CHUNK], BF16)
+                nc.sync.dma_start(out=ms_sb[:], in_=ms_dram[slots].partition_broadcast(P))
+
+                transpose_values(load_values(j * PASSES_PER_CHUNK), early[j])
+
+                for s in range(PASSES_PER_CHUNK):
+                    cols = slice(s * K_PASS, (s + 1) * K_PASS)
+                    mk_cols = mk_sb[:, cols].rearrange("c (m e) -> c e m", e=2)
+                    m2_cols = m2_sb[:, cols].rearrange("c (m e) -> c e m", e=2)
+                    ms_cols = ms_sb[:, cols].rearrange("c (m e) -> c e m", e=2)
+                    for pt in range(PIX_TILES):
+                        pixels = slice(pt * P, (pt + 1) * P)
+                        u = psum_sim.tile([P, 2, K_PASS // 2], F32, tag="u")
+                        nc.tensor.matmul(
+                            u[:], lhsT=qs_twice[:, pixels], rhs=mk_cols, start=True, stop=False
+                        )
+                        nc.tensor.matmul(
+                            u[:], lhsT=qe_minus[:, pixels], rhs=m2_cols, start=False, stop=True
+                        )
+                        nc.vector.scalar_tensor_tensor(
+                            out=w[pt][j][:, cols].rearrange("p (e m) -> p e m", e=2),
+                            in0=u[:],
+                            scalar=b_sq[:, pt : pt + 1],
+                            in1=ms_cols,
+                            op0=ALU.subtract,
+                            op1=ALU.mult,
+                        )
+                for pt in range(PIX_TILES):
+                    nc.vector.reduce_max(
+                        out=chunk_max[:, pt, j : j + 1], in_=w[pt][j][:], axis=AXIS.X
+                    )
+
+        w_max = const.tile([P, PIX_TILES], F32)
+        nc.vector.reduce_max(out=w_max[:], in_=chunk_max[:], axis=AXIS.X)
+        shift = const.tile([P, PIX_TILES], F32)
+        nc.vector.tensor_scalar(
+            out=shift[:], in0=w_max[:], scalar1=-INV_SQRT_CK, scalar2=None, op0=ALU.mult
+        )
+
+        psum_acc = whole.enter_context(tc.psum_pool(name="psum_acc", bufs=1))
+        acc = [psum_acc.tile([P, VAL], F32, name="acc%d" % pt) for pt in range(PIX_TILES)]
+
+        with ExitStack() as phase:
+            e_pool = phase.enter_context(tc.tile_pool(name="e", bufs=2))
+            mx_pool = phase.enter_context(tc.tile_pool(name="mx", bufs=3))
+            psum_e = phase.enter_context(tc.psum_pool(name="psum_e", bufs=2))
+
+            e_sb = {}
+            e_grouped = {}
+            mv_grouped = {}
+
+            def exponential(pt, j):
+                e_sb[(pt, j)] = e_pool.tile([P, CHUNK], BF16, name="e%d" % pt, tag="e%d" % pt)
+                nc.scalar.activation(
+                    out=e_sb[(pt, j)][:],
+                    in_=w[pt][j][:],
+                    func=ACT.Exp,
+                    bias=shift[:, pt : pt + 1],
+                    scale=INV_SQRT_CK,
+                    accum_out=chunk_sum[:, pt, j : j + 1],
+                )
+
+            def transposes(g):
+                j, s = divmod(g, PASSES_PER_CHUNK)
+                if s == 0 and j + 1 < CHUNKS:
+                    exponential(0, j + 1)
+                if s == PASSES_PER_CHUNK // 2 and j + 1 < CHUNKS:
+                    exponential(1, j + 1)
+
+                bank = psum_e.tile([P, 4, PIX], BF16)
+                for pt in range(PIX_TILES):
+                    for e in range(2):
+                        for u in range(2):
+                            first = s * K_PASS + e * (K_PASS // 2) + u * P
+                            nc.tensor.transpose(
+                                bank[:, 2 * u + e, pt * P : (pt + 1) * P],
+                                e_sb[(pt, j)][:, first : first + P],
+                                ident_bf16[:],
+                            )
+                e_four = grouped_pool.tile([P, PIX, 4], BF16, align_bytes=64)
+                nc.vector.tensor_copy(out=e_four[:], in_=bank[:].rearrange("i t p -> i p t"))
+                e_grouped[g] = e_four
+
+                if s == 0:
+                    mv_grouped[g] = early[j]
+                else:
+                    mv_four = grouped_pool.tile([P, 2 * VAL], F32, align_bytes=64)
+                    transpose_values(load_values(g), mv_four)
+                    mv_grouped[g] = mv_four
+
+            def readout(g):
+                e_codes = mx_pool.tile([P, PIX], U32, align_bytes=64)
+                e_scales = mx_pool.tile([P, PIX], U8, align_bytes=64)
+                nc.vector.quantize_mx(
+                    out=e_codes[:].bitcast(FP8X4),
+                    scales=e_scales[:],
+                    in_=e_grouped[g][:].rearrange("i p t -> i (p t)"),
+                )
+                mv_codes = mx_pool.tile([P, VAL], U32, align_bytes=64)
+                mv_scales = mx_pool.tile([P, VAL], U8, align_bytes=64)
+                nc.vector.quantize_mx(
+                    out=mv_codes[:].bitcast(FP8X4),
+                    scales=mv_scales[:],
+                    in_=mv_grouped[g][:].bitcast(BF16),
+                )
+                for pt in range(PIX_TILES):
+                    pixels = slice(pt * P, (pt + 1) * P)
+                    nc.tensor.matmul_mx(
+                        out=acc[pt][:],
+                        lhsT=e_codes[:, pixels].bitcast(FP8X4),
+                        lhsT_scale=e_scales[:, pixels],
+                        rhs=mv_codes[:].bitcast(FP8X4),
+                        rhs_scale=mv_scales[:],
+                        start=(g == 0),
+                        stop=(g == PASSES - 1),
+                    )
+
+            for pt in range(PIX_TILES):
+                exponential(pt, 0)
+            for step in range(PASSES + LEAD):
+                if step < PASSES:
+                    transposes(step)
+                if step >= LEAD:
+                    readout(step - LEAD)
+
+        with tc.tile_pool(name="tail", bufs=2) as tail:
+            total = const.tile([P, PIX_TILES], F32)
+            nc.vector.reduce_sum(out=total[:], in_=chunk_sum[:], axis=AXIS.X)
+            inv_total = const.tile([P, PIX_TILES], F32)
+            nc.vector.reciprocal(out=inv_total[:], in_=total[:])
+
+            mem0 = tail.tile([P, VAL], F32)
+            nc.vector.tensor_scalar(
+                out=mem0[:], in0=acc[0][:], scalar1=inv_total[:, 0:1], scalar2=None, op0=ALU.mult
+            )
+            mem1 = tail.tile([P, VAL], F32)
+            nc.scalar.activation(
+                out=mem1[:], in_=acc[1][:], func=ACT.Copy, scale=inv_total[:, 1:2]
+            )
+            mem = [mem0, mem1]
+            for h in range(VAL // HALF_VAL):
+                bank = psum_val.tile([P, 2, PIX], F32)
+                for q in range(2):
+                    channels = slice((2 * h + q) * P, (2 * h + q + 1) * P)
+                    for pt in range(PIX_TILES):
+                        nc.tensor.transpose(
+                            bank[:, q, pt * P : (pt + 1) * P], mem[pt][:, channels], ident_f32[:]
+                        )
+                result = tail.tile([P, 2, PIX], F32)
+                if h == 0:
+                    nc.vector.tensor_copy(out=result[:], in_=bank[:])
+                else:
+                    nc.scalar.copy(out=result[:], in_=bank[:])
+                nc.sync.dma_start(out=out_dram[:, 2 * h : 2 * h + 2, :], in_=result[:])

@@ -116,7 +116,8 @@ def tile_xmem_pa_k_kernel(
             for pt in range(PIX_TILES)
         ]
         chunk_max = const.tile([P, PIX_TILES, CHUNKS], F32)
-        chunk_sum = const.tile([P, PIX_TILES, CHUNKS], F32)
+        e_sums = const.tile([P, PIX_TILES, PASSES], F32)
+        nc.vector.memset(e_sums[:], 0.0)
         early = [
             early_pool.tile([P, 2 * VAL], F32, name="early%d" % j, align_bytes=64)
             for j in range(CHUNKS)
@@ -137,6 +138,10 @@ def tile_xmem_pa_k_kernel(
                 )
             b_sq = const.tile([P, PIX_TILES], F32)
             nc.vector.reduce_sum(out=b_sq[:], in_=b_bank[:], axis=AXIS.X)
+            b_minus = const.tile([P, PIX_TILES], F32)
+            nc.vector.tensor_scalar(
+                out=b_minus[:], in0=b_sq[:], scalar1=-1.0, scalar2=None, op0=ALU.mult
+            )
 
             for j in range(CHUNKS):
                 slots = slice(j * CHUNK, (j + 1) * CHUNK)
@@ -146,8 +151,7 @@ def tile_xmem_pa_k_kernel(
                 nc.sync.dma_start(out=m2_sb[:], in_=m2_dram[:, slots])
                 ms_sb = stream.tile([P, CHUNK], BF16)
                 nc.sync.dma_start(out=ms_sb[:], in_=ms_dram[slots].partition_broadcast(P))
-
-                transpose_values(load_values(j * PASSES_PER_CHUNK), early[j])
+                raw = load_values(j * PASSES_PER_CHUNK)
 
                 for s in range(PASSES_PER_CHUNK):
                     cols = slice(s * K_PASS, (s + 1) * K_PASS)
@@ -163,18 +167,32 @@ def tile_xmem_pa_k_kernel(
                         nc.tensor.matmul(
                             u[:], lhsT=qe_minus[:, pixels], rhs=m2_cols, start=False, stop=True
                         )
-                        nc.vector.scalar_tensor_tensor(
-                            out=w[pt][j][:, cols].rearrange("p (e m) -> p e m", e=2),
-                            in0=u[:],
-                            scalar=b_sq[:, pt : pt + 1],
-                            in1=ms_cols,
-                            op0=ALU.subtract,
-                            op1=ALU.mult,
-                        )
-                for pt in range(PIX_TILES):
+                        w_cols = w[pt][j][:, cols].rearrange("p (e m) -> p e m", e=2)
+                        if pt == 0:
+                            nc.vector.scalar_tensor_tensor(
+                                out=w_cols,
+                                in0=u[:],
+                                scalar=b_sq[:, pt : pt + 1],
+                                in1=ms_cols,
+                                op0=ALU.subtract,
+                                op1=ALU.mult,
+                            )
+                        else:
+                            nc.scalar.activation(
+                                out=w_cols, in_=u[:], func=ACT.Identity, bias=b_minus[:, pt : pt + 1]
+                            )
+                            nc.gpsimd.tensor_tensor(
+                                out=w_cols, in0=w_cols, in1=ms_cols, op=ALU.mult
+                            )
+                transpose_values(raw, early[j])
+                nc.vector.reduce_max(out=chunk_max[:, 0, j : j + 1], in_=w[0][j][:], axis=AXIS.X)
+                if j > 0:
                     nc.vector.reduce_max(
-                        out=chunk_max[:, pt, j : j + 1], in_=w[pt][j][:], axis=AXIS.X
+                        out=chunk_max[:, 1, j - 1 : j], in_=w[1][j - 1][:], axis=AXIS.X
                     )
+            nc.vector.reduce_max(
+                out=chunk_max[:, 1, CHUNKS - 1 : CHUNKS], in_=w[1][CHUNKS - 1][:], axis=AXIS.X
+            )
 
         w_max = const.tile([P, PIX_TILES], F32)
         nc.vector.reduce_max(out=w_max[:], in_=chunk_max[:], axis=AXIS.X)
@@ -195,23 +213,28 @@ def tile_xmem_pa_k_kernel(
             e_grouped = {}
             mv_grouped = {}
 
-            def exponential(pt, j):
-                e_sb[(pt, j)] = e_pool.tile([P, CHUNK], BF16, name="e%d" % pt, tag="e%d" % pt)
+            def exponential(pt, j, first, count):
+                if first == 0:
+                    e_sb[(pt, j)] = e_pool.tile(
+                        [P, CHUNK], BF16, name="e%d" % pt, tag="e%d" % pt
+                    )
+                cols = slice(first * K_PASS, (first + count) * K_PASS)
+                g = j * PASSES_PER_CHUNK + first
                 nc.scalar.activation(
-                    out=e_sb[(pt, j)][:],
-                    in_=w[pt][j][:],
+                    out=e_sb[(pt, j)][:, cols],
+                    in_=w[pt][j][:, cols],
                     func=ACT.Exp,
                     bias=shift[:, pt : pt + 1],
                     scale=INV_SQRT_CK,
-                    accum_out=chunk_sum[:, pt, j : j + 1],
+                    accum_out=e_sums[:, pt, g : g + 1],
                 )
 
             def transposes(g):
                 j, s = divmod(g, PASSES_PER_CHUNK)
                 if s == 0 and j + 1 < CHUNKS:
-                    exponential(0, j + 1)
+                    exponential(0, j + 1, 0, PASSES_PER_CHUNK)
                 if s == PASSES_PER_CHUNK // 2 and j + 1 < CHUNKS:
-                    exponential(1, j + 1)
+                    exponential(1, j + 1, 0, PASSES_PER_CHUNK)
 
                 bank = psum_e.tile([P, 4, PIX], BF16)
                 for pt in range(PIX_TILES):
@@ -262,7 +285,9 @@ def tile_xmem_pa_k_kernel(
                     )
 
             for pt in range(PIX_TILES):
-                exponential(pt, 0)
+                exponential(pt, 0, 0, 1)
+            for pt in range(PIX_TILES):
+                exponential(pt, 0, 1, PASSES_PER_CHUNK - 1)
             for step in range(PASSES + LEAD):
                 if step < PASSES:
                     transposes(step)
@@ -271,7 +296,7 @@ def tile_xmem_pa_k_kernel(
 
         with tc.tile_pool(name="tail", bufs=2) as tail:
             total = const.tile([P, PIX_TILES], F32)
-            nc.vector.reduce_sum(out=total[:], in_=chunk_sum[:], axis=AXIS.X)
+            nc.vector.reduce_sum(out=total[:], in_=e_sums[:], axis=AXIS.X)
             inv_total = const.tile([P, PIX_TILES], F32)
             nc.vector.reciprocal(out=inv_total[:], in_=total[:])
 

@@ -57,6 +57,7 @@ def tile_xmem_pa_k_kernel(
     out_dram = out.rearrange("b o c h w -> (b o c) (h w)").rearrange("(q r) p -> r q p", r=P)
 
     with ExitStack() as whole:
+        whole.enter_context(tc.manual_schedule())
         const = whole.enter_context(tc.tile_pool(name="const", bufs=1))
         sim_pool = whole.enter_context(tc.tile_pool(name="sim", bufs=1))
         early_pool = whole.enter_context(tc.tile_pool(name="early", bufs=1))

@@ -26,7 +26,9 @@ PASSES = SLOTS // K_PASS
 CHUNK = 2048
 CHUNKS = SLOTS // CHUNK
 PASSES_PER_CHUNK = CHUNK // K_PASS
-LEAD = 2
+PAIR = 2 * K_PASS
+PAIRS = SLOTS // PAIR
+PAIRS_PER_CHUNK = CHUNK // PAIR
 INV_SQRT_CK = 1.0 / math.sqrt(CK)
 
 FLOPS = 2 * SLOTS * PIX * (2 * CK + VAL)
@@ -57,7 +59,6 @@ def tile_xmem_pa_k_kernel(
     out_dram = out.rearrange("b o c h w -> (b o c) (h w)").rearrange("(q r) p -> r q p", r=P)
 
     with ExitStack() as whole:
-        whole.enter_context(tc.manual_schedule())
         const = whole.enter_context(tc.tile_pool(name="const", bufs=1))
         sim_pool = whole.enter_context(tc.tile_pool(name="sim", bufs=1))
         early_pool = whole.enter_context(tc.tile_pool(name="early", bufs=1))
@@ -95,8 +96,8 @@ def tile_xmem_pa_k_kernel(
             nc.sync.dma_start(out=raw[:], in_=mv_dram[:, :, g * K_PASS : (g + 1) * K_PASS])
             return raw
 
-        def transpose_values(raw, grouped):
-            pairs = grouped[:].rearrange("i (v u) -> i v u", u=2)
+        def transpose_values(raw):
+            banks = []
             for h in range(VAL // HALF_VAL):
                 bank = psum_val.tile([P, 2, HALF_VAL], F32)
                 for u in range(2):
@@ -107,9 +108,15 @@ def tile_xmem_pa_k_kernel(
                             words[:, u * P : (u + 1) * P],
                             ident_f32[:],
                         )
+                banks.append(bank)
+            return banks
+
+        def copy_values(banks, grouped):
+            pairs = grouped[:].rearrange("i (v u) -> i v u", u=2)
+            for h in range(VAL // HALF_VAL):
                 nc.scalar.copy(
                     out=pairs[:, h * HALF_VAL : (h + 1) * HALF_VAL, :],
-                    in_=bank[:].rearrange("i u v -> i v u"),
+                    in_=banks[h][:].rearrange("i u v -> i v u"),
                 )
 
         w = [
@@ -185,7 +192,7 @@ def tile_xmem_pa_k_kernel(
                             nc.gpsimd.tensor_tensor(
                                 out=w_cols, in0=w_cols, in1=ms_cols, op=ALU.mult
                             )
-                transpose_values(raw, early[j])
+                copy_values(transpose_values(raw), early[j])
                 nc.vector.reduce_max(out=chunk_max[:, 0, j : j + 1], in_=w[0][j][:], axis=AXIS.X)
                 if j > 0:
                     nc.vector.reduce_max(
@@ -206,24 +213,28 @@ def tile_xmem_pa_k_kernel(
         acc = [psum_acc.tile([P, VAL], F32, name="acc%d" % pt) for pt in range(PIX_TILES)]
 
         with ExitStack() as phase:
-            e_pool = phase.enter_context(tc.tile_pool(name="e", bufs=2))
+            phase.enter_context(tc.manual_schedule())
+            e_pool = phase.enter_context(tc.tile_pool(name="e", bufs=3))
             mx_pool = phase.enter_context(tc.tile_pool(name="mx", bufs=3))
             psum_e = phase.enter_context(tc.psum_pool(name="psum_e", bufs=2))
 
             e_sb = {}
+            e_banks = {}
+            mv_banks = {}
             e_grouped = {}
             mv_grouped = {}
+            codes = {}
 
-            def exponential(pt, j, first, count):
+            def exponential(pt, q, first, count):
                 if first == 0:
-                    e_sb[(pt, j)] = e_pool.tile(
-                        [P, CHUNK], BF16, name="e%d" % pt, tag="e%d" % pt
-                    )
+                    e_sb[(pt, q)] = e_pool.tile([P, PAIR], BF16, name="e%d" % pt, tag="e%d" % pt)
+                j, half = divmod(q, PAIRS_PER_CHUNK)
                 cols = slice(first * K_PASS, (first + count) * K_PASS)
-                g = j * PASSES_PER_CHUNK + first
+                w_cols = slice(half * PAIR + first * K_PASS, half * PAIR + (first + count) * K_PASS)
+                g = 2 * q + first
                 nc.scalar.activation(
-                    out=e_sb[(pt, j)][:, cols],
-                    in_=w[pt][j][:, cols],
+                    out=e_sb[(pt, q)][:, cols],
+                    in_=w[pt][j][:, w_cols],
                     func=ACT.Exp,
                     bias=shift[:, pt : pt + 1],
                     scale=INV_SQRT_CK,
@@ -231,12 +242,7 @@ def tile_xmem_pa_k_kernel(
                 )
 
             def transposes(g):
-                j, s = divmod(g, PASSES_PER_CHUNK)
-                if s == 0 and j + 1 < CHUNKS:
-                    exponential(0, j + 1, 0, PASSES_PER_CHUNK)
-                if s == PASSES_PER_CHUNK // 2 and j + 1 < CHUNKS:
-                    exponential(1, j + 1, 0, PASSES_PER_CHUNK)
-
+                q, s = divmod(g, 2)
                 bank = psum_e.tile([P, 4, PIX], BF16)
                 for pt in range(PIX_TILES):
                     for e in range(2):
@@ -244,21 +250,27 @@ def tile_xmem_pa_k_kernel(
                             first = s * K_PASS + e * (K_PASS // 2) + u * P
                             nc.tensor.transpose(
                                 bank[:, 2 * u + e, pt * P : (pt + 1) * P],
-                                e_sb[(pt, j)][:, first : first + P],
+                                e_sb[(pt, q)][:, first : first + P],
                                 ident_bf16[:],
                             )
-                e_four = grouped_pool.tile([P, PIX, 4], BF16, align_bytes=64)
-                nc.vector.tensor_copy(out=e_four[:], in_=bank[:].rearrange("i t p -> i p t"))
-                e_grouped[g] = e_four
+                e_banks[g] = bank
+                if g % PASSES_PER_CHUNK != 0:
+                    mv_banks[g] = transpose_values(load_values(g))
 
-                if s == 0:
-                    mv_grouped[g] = early[j]
+            def copies(g):
+                e_four = grouped_pool.tile([P, PIX, 4], BF16, align_bytes=64)
+                nc.vector.tensor_copy(
+                    out=e_four[:], in_=e_banks[g][:].rearrange("i t p -> i p t")
+                )
+                e_grouped[g] = e_four
+                if g % PASSES_PER_CHUNK == 0:
+                    mv_grouped[g] = early[g // PASSES_PER_CHUNK]
                 else:
                     mv_four = grouped_pool.tile([P, 2 * VAL], F32, align_bytes=64)
-                    transpose_values(load_values(g), mv_four)
+                    copy_values(mv_banks[g], mv_four)
                     mv_grouped[g] = mv_four
 
-            def readout(g):
+            def quantise(g):
                 e_codes = mx_pool.tile([P, PIX], U32, align_bytes=64)
                 e_scales = mx_pool.tile([P, PIX], U8, align_bytes=64)
                 nc.vector.quantize_mx(
@@ -273,6 +285,10 @@ def tile_xmem_pa_k_kernel(
                     scales=mv_scales[:],
                     in_=mv_grouped[g][:].bitcast(BF16),
                 )
+                codes[g] = (e_codes, e_scales, mv_codes, mv_scales)
+
+            def readout(g):
+                e_codes, e_scales, mv_codes, mv_scales = codes[g]
                 for pt in range(PIX_TILES):
                     pixels = slice(pt * P, (pt + 1) * P)
                     nc.tensor.matmul_mx(
@@ -285,15 +301,21 @@ def tile_xmem_pa_k_kernel(
                         stop=(g == PASSES - 1),
                     )
 
-            for pt in range(PIX_TILES):
-                exponential(pt, 0, 0, 1)
-            for pt in range(PIX_TILES):
-                exponential(pt, 0, 1, PASSES_PER_CHUNK - 1)
-            for step in range(PASSES + LEAD):
-                if step < PASSES:
-                    transposes(step)
-                if step >= LEAD:
-                    readout(step - LEAD)
+            for first in range(2):
+                for pt in range(PIX_TILES):
+                    exponential(pt, 0, first, 1)
+            exponential(0, 1, 0, 2)
+            for k in range(PASSES + 3):
+                if k < PASSES:
+                    transposes(k)
+                if 1 <= k <= PASSES:
+                    copies(k - 1)
+                if (k + 3) // 2 < PAIRS:
+                    exponential((k + 1) % 2, (k + 3) // 2, 0, 2)
+                if 2 <= k <= PASSES + 1:
+                    quantise(k - 2)
+                if k >= 3:
+                    readout(k - 3)
 
         with tc.tile_pool(name="tail", bufs=2) as tail:
             total = const.tile([P, PIX_TILES], F32)

@@ -29,6 +29,7 @@ PASSES_PER_CHUNK = CHUNK // K_PASS
 PAIR = 2 * K_PASS
 PAIRS = SLOTS // PAIR
 PAIRS_PER_CHUNK = CHUNK // PAIR
+FIRST_QUANTISED = 4
 INV_SQRT_CK = 1.0 / math.sqrt(CK)
 
 FLOPS = 2 * SLOTS * PIX * (2 * CK + VAL)
@@ -216,6 +217,7 @@ def tile_xmem_pa_k_kernel(
             phase.enter_context(tc.manual_schedule())
             e_pool = phase.enter_context(tc.tile_pool(name="e", bufs=3))
             mx_pool = phase.enter_context(tc.tile_pool(name="mx", bufs=3))
+            first_pool = phase.enter_context(tc.tile_pool(name="first", bufs=1))
             psum_e = phase.enter_context(tc.psum_pool(name="psum_e", bufs=2))
 
             e_sb = {}
@@ -223,6 +225,7 @@ def tile_xmem_pa_k_kernel(
             mv_banks = {}
             e_grouped = {}
             mv_grouped = {}
+            mv_quantised = {}
             codes = {}
 
             def exponential(pt, q, first, count):
@@ -270,6 +273,14 @@ def tile_xmem_pa_k_kernel(
                     copy_values(mv_banks[g], mv_four)
                     mv_grouped[g] = mv_four
 
+            def quantise_values(grouped, mv_codes, mv_scales):
+                nc.vector.quantize_mx(
+                    out=mv_codes[:].bitcast(FP8X4),
+                    scales=mv_scales[:],
+                    in_=grouped[:].bitcast(BF16),
+                )
+                return (mv_codes, mv_scales)
+
             def quantise(g):
                 e_codes = mx_pool.tile([P, PIX], U32, align_bytes=64)
                 e_scales = mx_pool.tile([P, PIX], U8, align_bytes=64)
@@ -278,14 +289,11 @@ def tile_xmem_pa_k_kernel(
                     scales=e_scales[:],
                     in_=e_grouped[g][:].rearrange("i p t -> i (p t)"),
                 )
-                mv_codes = mx_pool.tile([P, VAL], U32, align_bytes=64)
-                mv_scales = mx_pool.tile([P, VAL], U8, align_bytes=64)
-                nc.vector.quantize_mx(
-                    out=mv_codes[:].bitcast(FP8X4),
-                    scales=mv_scales[:],
-                    in_=mv_grouped[g][:].bitcast(BF16),
-                )
-                codes[g] = (e_codes, e_scales, mv_codes, mv_scales)
+                if g not in mv_quantised:
+                    mv_codes = mx_pool.tile([P, VAL], U32, align_bytes=64)
+                    mv_scales = mx_pool.tile([P, VAL], U8, align_bytes=64)
+                    mv_quantised[g] = quantise_values(mv_grouped[g], mv_codes, mv_scales)
+                codes[g] = (e_codes, e_scales) + mv_quantised[g]
 
             def readout(g):
                 e_codes, e_scales, mv_codes, mv_scales = codes[g]
@@ -305,6 +313,12 @@ def tile_xmem_pa_k_kernel(
                 for pt in range(PIX_TILES):
                     exponential(pt, 0, first, 1)
             exponential(0, 1, 0, 2)
+            for j in range(FIRST_QUANTISED):
+                mv_quantised[j * PASSES_PER_CHUNK] = quantise_values(
+                    early[j],
+                    first_pool.tile([P, VAL], U32, name="first_codes%d" % j, align_bytes=64),
+                    first_pool.tile([P, VAL], U8, name="first_scales%d" % j, align_bytes=64),
+                )
             for k in range(PASSES + 3):
                 if k < PASSES:
                     transposes(k)

@@ -29,7 +29,6 @@ PASSES_PER_CHUNK = CHUNK // K_PASS
 PAIR = 2 * K_PASS
 PAIRS = SLOTS // PAIR
 PAIRS_PER_CHUNK = CHUNK // PAIR
-FIRST_QUANTISED = 4
 INV_SQRT_CK = 1.0 / math.sqrt(CK)
 
 FLOPS = 2 * SLOTS * PIX * (2 * CK + VAL)
@@ -164,25 +163,22 @@ def tile_xmem_pa_k_kernel(
 
                 for s in range(PASSES_PER_CHUNK):
                     cols = slice(s * K_PASS, (s + 1) * K_PASS)
-                    mk_cols = mk_sb[:, cols].rearrange("c (m e) -> c e m", e=2)
-                    m2_cols = m2_sb[:, cols].rearrange("c (m e) -> c e m", e=2)
-                    ms_cols = ms_sb[:, cols].rearrange("c (m e) -> c e m", e=2)
                     for pt in range(PIX_TILES):
                         pixels = slice(pt * P, (pt + 1) * P)
-                        u = psum_sim.tile([P, 2, K_PASS // 2], F32, tag="u")
+                        u = psum_sim.tile([P, K_PASS], F32, tag="u")
                         nc.tensor.matmul(
-                            u[:], lhsT=qs_twice[:, pixels], rhs=mk_cols, start=True, stop=False
+                            u[:], lhsT=qs_twice[:, pixels], rhs=mk_sb[:, cols], start=True, stop=False
                         )
                         nc.tensor.matmul(
-                            u[:], lhsT=qe_minus[:, pixels], rhs=m2_cols, start=False, stop=True
+                            u[:], lhsT=qe_minus[:, pixels], rhs=m2_sb[:, cols], start=False, stop=True
                         )
-                        w_cols = w[pt][j][:, cols].rearrange("p (e m) -> p e m", e=2)
+                        w_cols = w[pt][j][:, cols]
                         if pt == 0:
                             nc.vector.scalar_tensor_tensor(
                                 out=w_cols,
                                 in0=u[:],
                                 scalar=b_sq[:, pt : pt + 1],
-                                in1=ms_cols,
+                                in1=ms_sb[:, cols],
                                 op0=ALU.subtract,
                                 op1=ALU.mult,
                             )
@@ -190,9 +186,14 @@ def tile_xmem_pa_k_kernel(
                             nc.scalar.activation(
                                 out=w_cols, in_=u[:], func=ACT.Identity, bias=b_minus[:, pt : pt + 1]
                             )
-                            nc.gpsimd.tensor_tensor(
-                                out=w_cols, in0=w_cols, in1=ms_cols, op=ALU.mult
-                            )
+                            if s % 2 == 1:
+                                both = slice((s - 1) * K_PASS, (s + 1) * K_PASS)
+                                nc.gpsimd.tensor_tensor(
+                                    out=w[pt][j][:, both],
+                                    in0=w[pt][j][:, both],
+                                    in1=ms_sb[:, both],
+                                    op=ALU.mult,
+                                )
                 copy_values(transpose_values(raw), early[j])
                 nc.vector.reduce_max(out=chunk_max[:, 0, j : j + 1], in_=w[0][j][:], axis=AXIS.X)
                 if j > 0:
@@ -217,7 +218,6 @@ def tile_xmem_pa_k_kernel(
             phase.enter_context(tc.manual_schedule())
             e_pool = phase.enter_context(tc.tile_pool(name="e", bufs=3))
             mx_pool = phase.enter_context(tc.tile_pool(name="mx", bufs=3))
-            first_pool = phase.enter_context(tc.tile_pool(name="first", bufs=1))
             psum_e = phase.enter_context(tc.psum_pool(name="psum_e", bufs=2))
 
             e_sb = {}
@@ -225,7 +225,6 @@ def tile_xmem_pa_k_kernel(
             mv_banks = {}
             e_grouped = {}
             mv_grouped = {}
-            mv_quantised = {}
             codes = {}
 
             def exponential(pt, q, first, count):
@@ -248,12 +247,12 @@ def tile_xmem_pa_k_kernel(
                 q, s = divmod(g, 2)
                 bank = psum_e.tile([P, 4, PIX], BF16)
                 for pt in range(PIX_TILES):
-                    for e in range(2):
-                        for u in range(2):
-                            first = s * K_PASS + e * (K_PASS // 2) + u * P
+                    for u in range(2):
+                        for e in range(2):
+                            first = s * K_PASS + u * 2 * P + e
                             nc.tensor.transpose(
                                 bank[:, 2 * u + e, pt * P : (pt + 1) * P],
-                                e_sb[(pt, q)][:, first : first + P],
+                                e_sb[(pt, q)][:, first : first + 2 * P - 1 : 2],
                                 ident_bf16[:],
                             )
                 e_banks[g] = bank
@@ -273,14 +272,6 @@ def tile_xmem_pa_k_kernel(
                     copy_values(mv_banks[g], mv_four)
                     mv_grouped[g] = mv_four
 
-            def quantise_values(grouped, mv_codes, mv_scales):
-                nc.vector.quantize_mx(
-                    out=mv_codes[:].bitcast(FP8X4),
-                    scales=mv_scales[:],
-                    in_=grouped[:].bitcast(BF16),
-                )
-                return (mv_codes, mv_scales)
-
             def quantise(g):
                 e_codes = mx_pool.tile([P, PIX], U32, align_bytes=64)
                 e_scales = mx_pool.tile([P, PIX], U8, align_bytes=64)
@@ -289,11 +280,14 @@ def tile_xmem_pa_k_kernel(
                     scales=e_scales[:],
                     in_=e_grouped[g][:].rearrange("i p t -> i (p t)"),
                 )
-                if g not in mv_quantised:
-                    mv_codes = mx_pool.tile([P, VAL], U32, align_bytes=64)
-                    mv_scales = mx_pool.tile([P, VAL], U8, align_bytes=64)
-                    mv_quantised[g] = quantise_values(mv_grouped[g], mv_codes, mv_scales)
-                codes[g] = (e_codes, e_scales) + mv_quantised[g]
+                mv_codes = mx_pool.tile([P, VAL], U32, align_bytes=64)
+                mv_scales = mx_pool.tile([P, VAL], U8, align_bytes=64)
+                nc.vector.quantize_mx(
+                    out=mv_codes[:].bitcast(FP8X4),
+                    scales=mv_scales[:],
+                    in_=mv_grouped[g][:].bitcast(BF16),
+                )
+                codes[g] = (e_codes, e_scales, mv_codes, mv_scales)
 
             def readout(g):
                 e_codes, e_scales, mv_codes, mv_scales = codes[g]
@@ -313,12 +307,6 @@ def tile_xmem_pa_k_kernel(
                 for pt in range(PIX_TILES):
                     exponential(pt, 0, first, 1)
             exponential(0, 1, 0, 2)
-            for j in range(FIRST_QUANTISED):
-                mv_quantised[j * PASSES_PER_CHUNK] = quantise_values(
-                    early[j],
-                    first_pool.tile([P, VAL], U32, name="first_codes%d" % j, align_bytes=64),
-                    first_pool.tile([P, VAL], U8, name="first_scales%d" % j, align_bytes=64),
-                )
             for k in range(PASSES + 3):
                 if k < PASSES:
                     transposes(k)

import math
from contextlib import ExitStack

import concourse.mybir as mybir
from concourse.masks import make_identity

F32 = mybir.dt.float32
BF16 = mybir.dt.bfloat16
U32 = mybir.dt.uint32
U8 = mybir.dt.uint8
FP8X4 = mybir.dt.float8_e4m3fn_x4
ALU = mybir.AluOpType
ACT = mybir.ActivationFunctionType
AXIS = mybir.AxisListType

P = 128
CK = 128
PIX = 256
PIX_TILES = PIX // P
SLOTS = 16384
VAL = 512
VAL_TILES = VAL // P
HALF_VAL = VAL // 2
K_PASS = 4 * P
PASSES = SLOTS // K_PASS
CHUNK = 2048
CHUNKS = SLOTS // CHUNK
PASSES_PER_CHUNK = CHUNK // K_PASS
PAIR = 2 * K_PASS
PAIRS = SLOTS // PAIR
PAIRS_PER_CHUNK = CHUNK // PAIR
INV_SQRT_CK = 1.0 / math.sqrt(CK)

FLOPS = 2 * SLOTS * PIX * (2 * CK + VAL)


def tile_xmem_pa_k_kernel(
    tc,
    query_key,
    query_selection,
    qk_sel,
    memory_key,
    mk_sq,
    memory_shrinkage,
    memory_value,
    out,
):
    nc = tc.nc

    qk_dram = query_key.rearrange("b c h w -> (b c) (h w)")
    qe_dram = query_selection.rearrange("b c h w -> (b c) (h w)")
    qs_dram = qk_sel.rearrange("b c h w -> (b c) (h w)")
    mk_dram = memory_key.rearrange("b c t h w -> (b c) (t h w)")
    m2_dram = mk_sq.rearrange("b c t h w -> (b c) (t h w)")
    ms_dram = memory_shrinkage.rearrange("b o t h w -> (b o t h w)")
    mv_dram = memory_value.rearrange("b o c t h w -> (b o c) (t h w)").rearrange(
        "(q r) n -> r q n", r=P
    )
    out_dram = out.rearrange("b o c h w -> (b o c) (h w)").rearrange("(q r) p -> r q p", r=P)

    with ExitStack() as whole:
        const = whole.enter_context(tc.tile_pool(name="const", bufs=1))
        sim_pool = whole.enter_context(tc.tile_pool(name="sim", bufs=1))
        early_pool = whole.enter_context(tc.tile_pool(name="early", bufs=1))
        raw_pool = whole.enter_context(tc.tile_pool(name="raw", bufs=4))
        grouped_pool = whole.enter_context(tc.tile_pool(name="grouped", bufs=3))
        psum_val = whole.enter_context(tc.psum_pool(name="psum_val", bufs=4))

        ident_f32 = const.tile([P, P], F32)
        make_identity(nc, ident_f32[:])
        ident_bf16 = const.tile([P, P], BF16)
        make_identity(nc, ident_bf16[:])

        warm = const.tile([P, 1], F32)
        nc.vector.memset(warm[:], 0.0)
        nc.scalar.activation(out=warm[:], in_=warm[:], func=ACT.Exp)

        qs_sb = const.tile([P, PIX], BF16)
        nc.sync.dma_start(out=qs_sb[:], in_=qs_dram)
        qe_sb = const.tile([P, PIX], BF16)
        nc.sync.dma_start(out=qe_sb[:], in_=qe_dram)
        qk_sb = const.tile([P, PIX], BF16)
        nc.sync.dma_start(out=qk_sb[:], in_=qk_dram)

        qs_twice = const.tile([P, PIX], BF16)
        nc.vector.tensor_scalar(
            out=qs_twice[:], in0=qs_sb[:], scalar1=2.0, scalar2=None, op0=ALU.mult
        )
        qe_minus = const.tile([P, PIX], BF16)
        nc.vector.tensor_scalar(
            out=qe_minus[:], in0=qe_sb[:], scalar1=-1.0, scalar2=None, op0=ALU.mult
        )

        def load_values(g):
            raw = raw_pool.tile([P, VAL_TILES, K_PASS], BF16)
            nc.sync.dma_start(out=raw[:], in_=mv_dram[:, :, g * K_PASS : (g + 1) * K_PASS])
            return raw

        def transpose_values(raw):
            banks = []
            for h in range(VAL // HALF_VAL):
                bank = psum_val.tile([P, 2, HALF_VAL], F32)
                for u in range(2):
                    for q in range(HALF_VAL // P):
                        words = raw[:, h * (HALF_VAL // P) + q, :].bitcast(F32)
                        nc.tensor.transpose(
                            bank[:, u, q * P : (q + 1) * P],
                            words[:, u * P : (u + 1) * P],
                            ident_f32[:],
                        )
                banks.append(bank)
            return banks

        def copy_values(banks, grouped):
            pairs = grouped[:].rearrange("i (v u) -> i v u", u=2)
            for h in range(VAL // HALF_VAL):
                nc.scalar.copy(
                    out=pairs[:, h * HALF_VAL : (h + 1) * HALF_VAL, :],
                    in_=banks[h][:].rearrange("i u v -> i v u"),
                )

        w = [
            [sim_pool.tile([P, CHUNK], F32, name="w%d_%d" % (pt, j)) for j in range(CHUNKS)]
            for pt in range(PIX_TILES)
        ]
        chunk_max = const.tile([P, PIX_TILES, CHUNKS], F32)
        e_sums = const.tile([P, PIX_TILES, PASSES], F32)
        nc.vector.memset(e_sums[:], 0.0)
        early = [
            early_pool.tile([P, 2 * VAL], F32, name="early%d" % j, align_bytes=64)
            for j in range(CHUNKS)
        ]

        with ExitStack() as phase:
            stream = phase.enter_context(tc.tile_pool(name="stream", bufs=2))
            psum_sim = phase.enter_context(tc.psum_pool(name="psum_sim", bufs=4))

            qk_sq = const.tile([P, PIX], F32)
            nc.vector.tensor_tensor(out=qk_sq[:], in0=qk_sb[:], in1=qk_sb[:], op=ALU.mult)
            b_terms = const.tile([P, PIX], F32)
            nc.vector.tensor_tensor(out=b_terms[:], in0=qk_sq[:], in1=qe_sb[:], op=ALU.mult)
            b_bank = psum_sim.tile([P, PIX_TILES, P], F32, tag="u")
            for pt in range(PIX_TILES):
                nc.tensor.transpose(
                    b_bank[:, pt, :], b_terms[:, pt * P : (pt + 1) * P], ident_f32[:]
                )
            b_sq = const.tile([P, PIX_TILES], F32)
            nc.vector.reduce_sum(out=b_sq[:], in_=b_bank[:], axis=AXIS.X)
            b_minus = const.tile([P, PIX_TILES], F32)
            nc.vector.tensor_scalar(
                out=b_minus[:], in0=b_sq[:], scalar1=-1.0, scalar2=None, op0=ALU.mult
            )

            for j in range(CHUNKS):
                slots = slice(j * CHUNK, (j + 1) * CHUNK)
                mk_sb = stream.tile([P, CHUNK], BF16)
                nc.sync.dma_start(out=mk_sb[:], in_=mk_dram[:, slots])
                m2_sb = stream.tile([P, CHUNK], BF16)
                nc.sync.dma_start(out=m2_sb[:], in_=m2_dram[:, slots])
                ms_sb = stream.tile([P, CHUNK], BF16)
                nc.sync.dma_start(out=ms_sb[:], in_=ms_dram[slots].partition_broadcast(P))
                raw = load_values(j * PASSES_PER_CHUNK)

                for s in range(PASSES_PER_CHUNK):
                    cols = slice(s * K_PASS, (s + 1) * K_PASS)
                    for pt in range(PIX_TILES):
                        pixels = slice(pt * P, (pt + 1) * P)
                        u = psum_sim.tile([P, K_PASS], F32, tag="u")
                        nc.tensor.matmul(
                            u[:], lhsT=qs_twice[:, pixels], rhs=mk_sb[:, cols], start=True, stop=False
                        )
                        nc.tensor.matmul(
                            u[:], lhsT=qe_minus[:, pixels], rhs=m2_sb[:, cols], start=False, stop=True
                        )
                        w_cols = w[pt][j][:, cols]
                        if pt == 0:
                            nc.vector.scalar_tensor_tensor(
                                out=w_cols,
                                in0=u[:],
                                scalar=b_sq[:, pt : pt + 1],
                                in1=ms_sb[:, cols],
                                op0=ALU.subtract,
                                op1=ALU.mult,
                            )
                        else:
                            nc.scalar.activation(
                                out=w_cols, in_=u[:], func=ACT.Identity, bias=b_minus[:, pt : pt + 1]
                            )
                            if s % 2 == 1:
                                both = slice((s - 1) * K_PASS, (s + 1) * K_PASS)
                                nc.gpsimd.tensor_tensor(
                                    out=w[pt][j][:, both],
                                    in0=w[pt][j][:, both],
                                    in1=ms_sb[:, both],
                                    op=ALU.mult,
                                )
                copy_values(transpose_values(raw), early[j])
                nc.vector.reduce_max(out=chunk_max[:, 0, j : j + 1], in_=w[0][j][:], axis=AXIS.X)
                if j > 0:
                    nc.vector.reduce_max(
                        out=chunk_max[:, 1, j - 1 : j], in_=w[1][j - 1][:], axis=AXIS.X
                    )
            nc.vector.reduce_max(
                out=chunk_max[:, 1, CHUNKS - 1 : CHUNKS], in_=w[1][CHUNKS - 1][:], axis=AXIS.X
            )

        w_max = const.tile([P, PIX_TILES], F32)
        nc.vector.reduce_max(out=w_max[:], in_=chunk_max[:], axis=AXIS.X)
        shift = const.tile([P, PIX_TILES], F32)
        nc.vector.tensor_scalar(
            out=shift[:], in0=w_max[:], scalar1=-INV_SQRT_CK, scalar2=None, op0=ALU.mult
        )

        psum_acc = whole.enter_context(tc.psum_pool(name="psum_acc", bufs=1))
        acc = [psum_acc.tile([P, VAL], F32, name="acc%d" % pt) for pt in range(PIX_TILES)]

        with ExitStack() as phase:
            phase.enter_context(tc.manual_schedule())
            e_pool = phase.enter_context(tc.tile_pool(name="e", bufs=3))
            mx_pool = phase.enter_context(tc.tile_pool(name="mx", bufs=3))
            psum_e = phase.enter_context(tc.psum_pool(name="psum_e", bufs=2))

            e_sb = {}
            e_banks = {}
            mv_banks = {}
            e_grouped = {}
            mv_grouped = {}
            codes = {}

            def exponential(pt, q, first, count):
                if first == 0:
                    e_sb[(pt, q)] = e_pool.tile([P, PAIR], BF16, name="e%d" % pt, tag="e%d" % pt)
                j, half = divmod(q, PAIRS_PER_CHUNK)
                cols = slice(first * K_PASS, (first + count) * K_PASS)
                w_cols = slice(half * PAIR + first * K_PASS, half * PAIR + (first + count) * K_PASS)
                g = 2 * q + first
                nc.scalar.activation(
                    out=e_sb[(pt, q)][:, cols],
                    in_=w[pt][j][:, w_cols],
                    func=ACT.Exp,
                    bias=shift[:, pt : pt + 1],
                    scale=INV_SQRT_CK,
                    accum_out=e_sums[:, pt, g : g + 1],
                )

            def transposes(g):
                q, s = divmod(g, 2)
                bank = psum_e.tile([P, 4, PIX], BF16)
                for pt in range(PIX_TILES):
                    for u in range(2):
                        for e in range(2):
                            first = s * K_PASS + u * 2 * P + e
                            nc.tensor.transpose(
                                bank[:, 2 * u + e, pt * P : (pt + 1) * P],
                                e_sb[(pt, q)][:, first : first + 2 * P - 1 : 2],
                                ident_bf16[:],
                            )
                e_banks[g] = bank
                if g % PASSES_PER_CHUNK != 0:
                    mv_banks[g] = transpose_values(load_values(g))

            def copies(g):
                e_four = grouped_pool.tile([P, PIX, 4], BF16, align_bytes=64)
                nc.vector.tensor_copy(
                    out=e_four[:], in_=e_banks[g][:].rearrange("i t p -> i p t")
                )
                e_grouped[g] = e_four
                if g % PASSES_PER_CHUNK == 0:
                    mv_grouped[g] = early[g // PASSES_PER_CHUNK]
                else:
                    mv_four = grouped_pool.tile([P, 2 * VAL], F32, align_bytes=64)
                    copy_values(mv_banks[g], mv_four)
                    mv_grouped[g] = mv_four

            def quantise(g):
                e_codes = mx_pool.tile([P, PIX], U32, align_bytes=64)
                e_scales = mx_pool.tile([P, PIX], U8, align_bytes=64)
                nc.vector.quantize_mx(
                    out=e_codes[:].bitcast(FP8X4),
                    scales=e_scales[:],
                    in_=e_grouped[g][:].rearrange("i p t -> i (p t)"),
                )
                mv_codes = mx_pool.tile([P, VAL], U32, align_bytes=64)
                mv_scales = mx_pool.tile([P, VAL], U8, align_bytes=64)
                nc.vector.quantize_mx(
                    out=mv_codes[:].bitcast(FP8X4),
                    scales=mv_scales[:],
                    in_=mv_grouped[g][:].bitcast(BF16),
                )
                codes[g] = (e_codes, e_scales, mv_codes, mv_scales)

            def readout(g):
                e_codes, e_scales, mv_codes, mv_scales = codes[g]
                for pt in range(PIX_TILES):
                    pixels = slice(pt * P, (pt + 1) * P)
                    nc.tensor.matmul_mx(
                        out=acc[pt][:],
                        lhsT=e_codes[:, pixels].bitcast(FP8X4),
                        lhsT_scale=e_scales[:, pixels],
                        rhs=mv_codes[:].bitcast(FP8X4),
                        rhs_scale=mv_scales[:],
                        start=(g == 0),
                        stop=(g == PASSES - 1),
                    )

            for first in range(2):
                for pt in range(PIX_TILES):
                    exponential(pt, 0, first, 1)
            exponential(0, 1, 0, 2)
            for k in range(PASSES + 3):
                if k < PASSES:
                    transposes(k)
                if 1 <= k <= PASSES:
                    copies(k - 1)
                if (k + 3) // 2 < PAIRS:
                    exponential((k + 1) % 2, (k + 3) // 2, 0, 2)
                if 2 <= k <= PASSES + 1:
                    quantise(k - 2)
                if k >= 3:
                    readout(k - 3)

        with tc.tile_pool(name="tail", bufs=2) as tail:
            total = const.tile([P, PIX_TILES], F32)
            nc.vector.reduce_sum(out=total[:], in_=e_sums[:], axis=AXIS.X)
            inv_total = const.tile([P, PIX_TILES], F32)
            nc.vector.reciprocal(out=inv_total[:], in_=total[:])

            mem0 = tail.tile([P, VAL], F32)
            nc.vector.tensor_scalar(
                out=mem0[:], in0=acc[0][:], scalar1=inv_total[:, 0:1], scalar2=None, op0=ALU.mult
            )
            mem1 = tail.tile([P, VAL], F32)
            nc.scalar.activation(
                out=mem1[:], in_=acc[1][:], func=ACT.Copy, scale=inv_total[:, 1:2]
            )
            mem = [mem0, mem1]
            for h in range(VAL // HALF_VAL):
                bank = psum_val.tile([P, 2, PIX], F32)
                for q in range(2):
                    channels = slice((2 * h + q) * P, (2 * h + q + 1) * P)
                    for pt in range(PIX_TILES):
                        nc.tensor.transpose(
                            bank[:, q, pt * P : (pt + 1) * P], mem[pt][:, channels], ident_f32[:]
                        )
                result = tail.tile([P, 2, PIX], F32)
                if h == 0:
                    nc.vector.tensor_copy(out=result[:], in_=bank[:])
                else:
                    nc.scalar.copy(out=result[:], in_=bank[:])
                nc.sync.dma_start(out=out_dram[:, 2 * h : 2 * h + 2, :], in_=result[:])
